import numpy as np
import ml_dtypes


def mxq(x, axis, fmt="e4m3"):
    dtype, down = {"e4m3": (ml_dtypes.float8_e4m3fn, 7), "e5m2": (ml_dtypes.float8_e5m2, 14)}[fmt]
    v = np.moveaxis(np.asarray(x, np.float32).astype(ml_dtypes.bfloat16).astype(np.float64), axis, -1)
    blocks = v.reshape(v.shape[:-1] + (-1, 32))
    amax = np.abs(blocks).max(-1, keepdims=True)
    byte = np.maximum(np.where(amax > 0, np.frexp(amax)[1] - 1 + 127, 0) - down, 1)
    scale = np.exp2(byte - 127.0)
    codes = (blocks / scale).astype(np.float32).astype(dtype).astype(np.float64)
    return np.moveaxis((codes * scale).reshape(v.shape), -1, axis)


WIDE = False


def mx_kscale(k):
    if not WIDE:
        return np.ones(k)
    levels = np.array([10, -10, 5, -5, 0])
    if k % 512:
        return np.exp2(np.random.permutation(np.resize(levels, k // 32))).repeat(32)
    a = np.empty((k // 512, 16))
    for p in range(k // 512):
        a[p, :8] = np.random.permutation(np.resize(levels, 8))
        for g in range(8):
            far = levels[np.abs(levels - a[p, g]) >= 10]
            a[p, g + 8] = far[np.random.randint(len(far))]
    return np.exp2(a.ravel()).repeat(32)


BF16 = ml_dtypes.bfloat16


def bf(x):
    return np.asarray(x, np.float32).astype(BF16)


def f64(x):
    return np.asarray(x).astype(np.float64)


B, S, H, D = 1, 1024, 16, 128
SOFT_CAP = 20.0
BLOCKED = -30000.0


def setup_inputs():
    s = mx_kscale(S)
    query = np.random.standard_normal((B, S, H, D)) * 1.5
    key = np.random.standard_normal((B, S, H, D)) * 1.5
    value = np.random.standard_normal((B, S, H, D)) * (s.max() / s)[None, :, None, None]
    bias = np.random.standard_normal((1, 1, S, S)) * 0.5 + np.log(s)[None, None, None, :]
    bias = np.where(np.random.random((1, 1, S, S)) < 0.25, BLOCKED, bias)
    return {"query": bf(query), "key": bf(key), "value": bf(value), "attn_mask": bf(bias)}


def reference(query, key, value, attn_mask):
    q = np.swapaxes(f64(query), 1, 2)
    k = np.swapaxes(f64(key), 1, 2)
    v = np.swapaxes(f64(value), 1, 2)
    scale = q.shape[-1] ** (-0.5)
    scores = (q @ np.swapaxes(k, 2, 3)) * scale
    scores = SOFT_CAP * np.tanh(scores / SOFT_CAP)
    scores = scores + f64(attn_mask)
    e = np.exp(scores - scores.max(-1, keepdims=True))
    out = (mxq(e, 3, "e4m3") @ mxq(v, 2, "e4m3")) / e.sum(-1, keepdims=True)
    return np.swapaxes(out, 1, 2)

@@ -1,0 +1,322 @@
+import math
+from contextlib import ExitStack
+
+import concourse.mybir as mybir
+from concourse.masks import make_identity
+
+F32 = mybir.dt.float32
+BF16 = mybir.dt.bfloat16
+U32 = mybir.dt.uint32
+U8 = mybir.dt.uint8
+FP8X4 = mybir.dt.float8_e4m3fn_x4
+ACT = mybir.ActivationFunctionType
+ALU = mybir.AluOpType
+
+P = 128
+S = 1024
+H = 16
+D = 128
+NT = S // P
+BANK = 512
+PACK = 4
+PASSES = S // (P * PACK)
+PAIRS_PER_HEAD = NT // 2
+NPAIR = H * PAIRS_PER_HEAD
+NBANK = 4 * NPAIR
+SOFT_CAP = 20.0
+FLOPS = 2 * 2 * H * S * S * D
+
+V_COLS = 320
+G_COLS = S - V_COLS
+
+MAX_LAG = 2
+EXP_LAG = 3
+COPY_LAG = 4
+QUANT_LAG = 5
+NORM_LAG = 6
+
+SBUF_DEPTH = {
+    "k_raw": 3,
+    "q_raw": 3,
+    "v_raw": 3,
+    "k_t": 2,
+    "q_t": 2,
+    "v_grouped": 2,
+    "v_words": 3,
+    "v_scales": 3,
+    "tanh_sb": 3,
+    "capped": EXP_LAG + 1,
+    "neg_max": 2,
+    "exp_bias": 2,
+    "e": 4,
+    "e_grouped": QUANT_LAG - EXP_LAG + 1,
+    "e_words": 2,
+    "e_scales": 2,
+    "row_sum": NORM_LAG - EXP_LAG + 1,
+    "row_inv": 2,
+    "out_sb": 2,
+}
+SCORE_BANKS = 3
+TRANSPOSE_BANKS = 4
+OUT_BANKS = 1
+
+
+def tile_naivesdpa_kernel(tc, query, key, value, attn_mask, out):
+    nc = tc.nc
+    q_rows = query.rearrange("b (j p) h d -> p (b j) h d", p=P)
+    k_rows = key.rearrange("b (g p t) h d -> p (b g) t h d", p=P, t=PACK)
+    v_rows = value.rearrange("b (g p t) h d -> p (b g) t h d", p=P, t=PACK)
+    bias_rows = attn_mask.rearrange("a b (j p) k -> p (a b j) k", p=P)
+    out_rows = out.rearrange("b (j p) h d -> p (b j) h d", p=P)
+    tanh_scale = 1.0 / (math.sqrt(D) * SOFT_CAP)
+
+    with ExitStack() as ctx:
+        sb = ctx.enter_context(tc.tile_pool(name="sb", bufs=1))
+        ps = ctx.enter_context(tc.psum_pool(name="ps", bufs=1))
+        ctx.enter_context(tc.manual_schedule())
+
+        k_raw, q_raw, v_raw, k_t, q_t, v_grouped, v_words, v_scales, out_sb = {}, {}, {}, {}, {}, {}, {}, {}, {}
+        scores, tanh_sb, capped, neg_max, exp_bias, e_t, e_grouped, e_words, e_scales = {}, {}, {}, {}, {}, {}, {}, {}, {}
+        row_sum, row_inv, out_ps = {}, {}, {}
+
+        def sbuf(tag, shape, dtype):
+            return sb.tile(shape, dtype, name=tag, tag=tag, bufs=SBUF_DEPTH[tag], align_bytes=64)
+
+        def load_head(store, rows, h, tag):
+            store[h] = sbuf(tag, [P, NT, D], BF16)
+            nc.sync.dma_start(out=store[h][:], in_=rows[:, :, h, :])
+
+        def load_keys(store, rows, h, tag):
+            store[h] = sbuf(tag, [P, NT, D], BF16)
+            for g in range(PASSES):
+                nc.sync.dma_start(out=store[h][:, PACK * g:PACK * (g + 1), :], in_=rows[:, g, :, h, :])
+
+        def transpose_head(raw):
+            bank = ps.tile([P, S], BF16, name="head_t", tag="t", bufs=TRANSPOSE_BANKS)
+            for j in range(NT):
+                nc.tensor.transpose(bank[:, j * P:(j + 1) * P], raw[:, j, :], ident[:])
+            return bank
+
+        def keep_head(store, bank, h, tag, copy):
+            store[h] = sbuf(tag, [P, S], BF16)
+            copy(out=store[h][:], in_=bank[:])
+
+        def group_v(h):
+            v_grouped[h] = sbuf("v_grouped", [P, S], BF16)
+            nc.vector.tensor_copy(
+                out=v_grouped[h][:].rearrange("p (g d t) -> p g d t", g=PASSES, t=PACK),
+                in_=v_raw[h][:].rearrange("p (g t) d -> p g d t", g=PASSES),
+            )
+
+        def quantise_v(h):
+            v_words[h] = sbuf("v_words", [P, PASSES * D], U32)
+            v_scales[h] = sbuf("v_scales", [P, PASSES * D], U8)
+            nc.vector.quantize_mx(out=v_words[h][:].bitcast(FP8X4), scales=v_scales[h][:], in_=v_grouped[h][:])
+
+        def scale_bias(j, mul):
+            mul(
+                b20[:, j, :].rearrange("q (g t p) -> q g t p", g=PASSES, t=PACK),
+                bias_raw[:, j, :].rearrange("q (g p t) -> q g t p", g=PASSES, t=PACK),
+                1.0 / SOFT_CAP,
+            )
+
+        def score_bank(x):
+            pair, b = divmod(x, 4)
+            h = pair // PAIRS_PER_HEAD
+            tile_no = 2 * (pair % PAIRS_PER_HEAD) + b // 2
+            half = b % 2
+            scores[x] = ps.tile([P, BANK], F32, name="scores", tag="scores", bufs=SCORE_BANKS)
+            nc.tensor.matmul(
+                scores[x][:],
+                lhsT=q_t[h][:, tile_no * P:(tile_no + 1) * P],
+                rhs=k_t[h][:, half * BANK:(half + 1) * BANK],
+                start=True,
+                stop=True,
+            )
+
+        def tanh_bank(x):
+            pair, b = divmod(x, 4)
+            half = b % 2
+            nc.scalar.activation(
+                out=tanh_sb[pair][:, b // 2, half * BANK:(half + 1) * BANK], in_=scores[x][:], func=ACT.Tanh, scale=tanh_scale
+            )
+            if x + SCORE_BANKS < NBANK:
+                score_bank(x + SCORE_BANKS)
+
+        def add_bias(pair, engine, cols):
+            j = 2 * (pair % PAIRS_PER_HEAD)
+            engine.tensor_tensor(
+                out=capped[pair][:, :, cols], in0=tanh_sb[pair][:, :, cols], in1=b20[:, j:j + 2, cols], op=ALU.add
+            )
+
+        def row_max(pair):
+            neg_max[pair] = sbuf("neg_max", [P, 2], F32)
+            nc.vector.tensor_reduce(
+                out=neg_max[pair][:], in_=capped[pair][:], axis=mybir.AxisListType.X, op=ALU.max, negate=True
+            )
+
+        def scale_max(pair):
+            exp_bias[pair] = sbuf("exp_bias", [P, 2], F32)
+            nc.gpsimd.tensor_scalar(
+                out=exp_bias[pair][:], in0=neg_max[pair][:], scalar1=SOFT_CAP, scalar2=0.0, op0=ALU.mult, op1=ALU.add
+            )
+
+        def exp_unit(pair, u):
+            if u == 0:
+                row_sum[pair] = sbuf("row_sum", [P, 2], F32)
+            e = sbuf("e", [P, S], BF16)
+            nc.scalar.activation(
+                out=e[:],
+                in_=capped[pair][:, u, :],
+                func=ACT.Exp,
+                bias=exp_bias[pair][:, u:u + 1],
+                scale=SOFT_CAP,
+                accum_out=row_sum[pair][:, u:u + 1],
+            )
+            e_t[(pair, u)] = ps.tile([P, S], BF16, name="e_t", tag="t", bufs=TRANSPOSE_BANKS)
+            for j in range(NT):
+                nc.tensor.transpose(e_t[(pair, u)][:, j * P:(j + 1) * P], e[:, j * P:(j + 1) * P], ident[:])
+
+        def group_e(pair, u, copy):
+            if u == 0:
+                e_grouped[pair] = sbuf("e_grouped", [P, 2, S], BF16)
+            copy(
+                out=e_grouped[pair][:, u, :].rearrange("p (g q t) -> p g q t", g=PASSES, t=PACK),
+                in_=e_t[(pair, u)][:].rearrange("p (g t q) -> p g q t", g=PASSES, t=PACK),
+            )
+
+        def quantise_e(pair):
+            e_words[pair] = sbuf("e_words", [P, 2 * PASSES * P], U32)
+            e_scales[pair] = sbuf("e_scales", [P, 2 * PASSES * P], U8)
+            nc.vector.quantize_mx(
+                out=e_words[pair][:].bitcast(FP8X4),
+                scales=e_scales[pair][:],
+                in_=e_grouped[pair][:].rearrange("p u c -> p (u c)"),
+            )
+
+        def e_times_v(pair):
+            h = pair // PAIRS_PER_HEAD
+            out_ps[pair] = ps.tile([P, 2, D], F32, name="out_ps", tag="out_ps", bufs=OUT_BANKS)
+            for u in range(2):
+                for g in range(PASSES):
+                    q_cols = slice((PASSES * u + g) * P, (PASSES * u + g + 1) * P)
+                    d_cols = slice(g * D, (g + 1) * D)
+                    nc.tensor.matmul_mx(
+                        out=out_ps[pair][:, u, :],
+                        lhsT=e_words[pair][:, q_cols].bitcast(FP8X4),
+                        lhsT_scale=e_scales[pair][:, q_cols],
+                        rhs=v_words[h][:, d_cols].bitcast(FP8X4),
+                        rhs_scale=v_scales[h][:, d_cols],
+                        start=(g == 0),
+                        stop=(g == PASSES - 1),
+                    )
+
+        def invert_sum(pair):
+            row_inv[pair] = sbuf("row_inv", [P, 2], F32)
+            nc.vector.reciprocal(row_inv[pair][:], row_sum[pair][:])
+
+        def divide_and_store(pair):
+            h, part = divmod(pair, PAIRS_PER_HEAD)
+            if part == 0:
+                out_sb[h] = sbuf("out_sb", [P, NT, D], F32)
+            nc.vector.tensor_tensor(
+                out=out_sb[h][:, 2 * part:2 * part + 2, :],
+                in0=out_ps[pair][:],
+                in1=row_inv[pair][:].unsqueeze(2).to_broadcast([P, 2, D]),
+                op=ALU.mult,
+            )
+            if part == PAIRS_PER_HEAD - 1:
+                nc.sync.dma_start(out=out_rows[:, :, h, :], in_=out_sb[h][:])
+
+        def live(pair):
+            return 0 <= pair < NPAIR
+
+        warm = sb.tile([P, 2], F32, name="warm", tag="warm")
+        nc.vector.memset(warm[:, 0:1], 0.0)
+        nc.scalar.activation(out=warm[:, 1:2], in_=warm[:, 0:1], func=ACT.Tanh)
+        bias_raw = sb.tile([P, NT, S], BF16, name="bias_raw", tag="bias_raw")
+        b20 = sb.tile([P, NT, S], F32, name="b20", tag="b20")
+        load_keys(k_raw, k_rows, 0, "k_raw")
+        load_head(q_raw, q_rows, 0, "q_raw")
+        nc.sync.dma_start(out=bias_raw[:, 0:2, :], in_=bias_rows[:, 0:2, :])
+        nc.sync.dma_start(out=bias_raw[:, 2:4, :], in_=bias_rows[:, 2:4, :])
+        load_keys(k_raw, k_rows, 1, "k_raw")
+        load_head(q_raw, q_rows, 1, "q_raw")
+        nc.sync.dma_start(out=bias_raw[:, 4:8, :], in_=bias_rows[:, 4:8, :])
+        load_keys(v_raw, v_rows, 0, "v_raw")
+        load_keys(v_raw, v_rows, 1, "v_raw")
+        ident = sb.tile([P, P], BF16, name="ident", tag="ident")
+        make_identity(nc, ident[:])
+        keep_head(k_t, transpose_head(k_raw[0]), 0, "k_t", nc.vector.tensor_copy)
+        keep_head(q_t, transpose_head(q_raw[0]), 0, "q_t", nc.scalar.copy)
+        scale_bias(0, nc.vector.tensor_scalar_mul)
+        scale_bias(1, nc.vector.tensor_scalar_mul)
+        for x in range(SCORE_BANKS):
+            score_bank(x)
+        waiting = {}
+
+        for n in range(NPAIR + NORM_LAG + 1):
+            h, part = divmod(n, PAIRS_PER_HEAD)
+            next_head = h + 1 if h + 1 < H else None
+
+            if live(n):
+                tanh_sb[n] = sbuf("tanh_sb", [P, 2, S], F32)
+                tanh_bank(4 * n)
+                tanh_bank(4 * n + 1)
+            if live(n - EXP_LAG):
+                exp_unit(n - EXP_LAG, 0)
+            if live(n):
+                tanh_bank(4 * n + 2)
+                tanh_bank(4 * n + 3)
+            if 1 <= n < PAIRS_PER_HEAD:
+                scale_bias(2 * n, nc.scalar.mul)
+                scale_bias(2 * n + 1, nc.scalar.mul)
+            if live(n - EXP_LAG):
+                exp_unit(n - EXP_LAG, 1)
+                group_e(n - EXP_LAG, 0, nc.scalar.copy)
+
+            if live(n - MAX_LAG):
+                row_max(n - MAX_LAG)
+            if live(n - QUANT_LAG):
+                quantise_e(n - QUANT_LAG)
+            if live(n - NORM_LAG):
+                invert_sum(n - NORM_LAG)
+            if live(n):
+                capped[n] = sbuf("capped", [P, 2, S], F32)
+                add_bias(n, nc.vector, slice(G_COLS, S))
+            if part == 2:
+                if h == 0:
+                    group_v(0)
+                if next_head is not None:
+                    group_v(next_head)
+            if part == 3:
+                if h == 0:
+                    quantise_v(0)
+                if next_head is not None:
+                    quantise_v(next_head)
+
+            if live(n - MAX_LAG):
+                scale_max(n - MAX_LAG)
+            if live(n):
+                add_bias(n, nc.gpsimd, slice(0, G_COLS))
+
+            if live(n - NORM_LAG):
+                divide_and_store(n - NORM_LAG)
+            if live(n - QUANT_LAG):
+                e_times_v(n - QUANT_LAG)
+            if live(n - COPY_LAG):
+                group_e(n - COPY_LAG, 1, nc.vector.tensor_copy)
+
+            if next_head is not None:
+                if part == 1:
+                    keep_head(k_t, waiting["k"], next_head, "k_t", nc.vector.tensor_copy)
+                if part == 2:
+                    keep_head(q_t, waiting["q"], next_head, "q_t", nc.vector.tensor_copy)
+                if part == 0:
+                    waiting["k"] = transpose_head(k_raw[next_head])
+                if part == 1:
+                    waiting["q"] = transpose_head(q_raw[next_head])
+            if part == 1 and h + 2 < H:
+                load_keys(k_raw, k_rows, h + 2, "k_raw")
+                load_head(q_raw, q_rows, h + 2, "q_raw")
+                load_keys(v_raw, v_rows, h + 2, "v_raw")

@@ -20,6 +20,7 @@ NT = S // P
 BANK = 512
 PACK = 4
 PASSES = S // (P * PACK)
+WORDS = S // 2
 PAIRS_PER_HEAD = NT // 2
 NPAIR = H * PAIRS_PER_HEAD
 NBANK = 4 * NPAIR
@@ -64,7 +65,7 @@ OUT_BANKS = 1
 def tile_naivesdpa_kernel(tc, query, key, value, attn_mask, out):
     nc = tc.nc
     q_rows = query.rearrange("b (j p) h d -> p (b j) h d", p=P)
-    k_rows = key.rearrange("b (g p t) h d -> p (b g) t h d", p=P, t=PACK)
+    k_rows = key.rearrange("b (j p) h d -> p (b j) h d", p=P)
     v_rows = value.rearrange("b (g p t) h d -> p (b g) t h d", p=P, t=PACK)
     bias_rows = attn_mask.rearrange("a b (j p) k -> p (a b j) k", p=P)
     out_rows = out.rearrange("b (j p) h d -> p (b j) h d", p=P)
@@ -114,11 +115,7 @@ def tile_naivesdpa_kernel(tc, query, key, value, attn_mask, out):
             nc.vector.quantize_mx(out=v_words[h][:].bitcast(FP8X4), scales=v_scales[h][:], in_=v_grouped[h][:])
 
         def scale_bias(j, mul):
-            mul(
-                b20[:, j, :].rearrange("q (g t p) -> q g t p", g=PASSES, t=PACK),
-                bias_raw[:, j, :].rearrange("q (g p t) -> q g t p", g=PASSES, t=PACK),
-                1.0 / SOFT_CAP,
-            )
+            mul(b20[:, j, :], bias_raw[:, j, :], 1.0 / SOFT_CAP)
 
         def score_bank(x):
             pair, b = divmod(x, 4)
@@ -173,16 +170,21 @@ def tile_naivesdpa_kernel(tc, query, key, value, attn_mask, out):
                 scale=SOFT_CAP,
                 accum_out=row_sum[pair][:, u:u + 1],
             )
-            e_t[(pair, u)] = ps.tile([P, S], BF16, name="e_t", tag="t", bufs=TRANSPOSE_BANKS)
-            for j in range(NT):
-                nc.tensor.transpose(e_t[(pair, u)][:, j * P:(j + 1) * P], e[:, j * P:(j + 1) * P], ident[:])
+            e_t[(pair, u)] = ps.tile([P, WORDS], F32, name="e_t", tag="t", bufs=TRANSPOSE_BANKS)
+            words = e[:].bitcast(F32)
+            for g in range(PASSES):
+                for i in range(2):
+                    block = 2 * g + i
+                    nc.tensor.transpose(
+                        e_t[(pair, u)][:, block * P:(block + 1) * P], words[:, 2 * P * g + i:2 * P * (g + 1):2], ident_f32[:]
+                    )
 
         def group_e(pair, u, copy):
             if u == 0:
                 e_grouped[pair] = sbuf("e_grouped", [P, 2, S], BF16)
             copy(
-                out=e_grouped[pair][:, u, :].rearrange("p (g q t) -> p g q t", g=PASSES, t=PACK),
-                in_=e_t[(pair, u)][:].rearrange("p (g t q) -> p g q t", g=PASSES, t=PACK),
+                out=e_grouped[pair][:, u, :].bitcast(F32).rearrange("p (g q i) -> p g q i", g=PASSES, i=2),
+                in_=e_t[(pair, u)][:].rearrange("p (g i q) -> p g q i", g=PASSES, i=2),
             )
 
         def quantise_e(pair):
@@ -236,17 +238,19 @@ def tile_naivesdpa_kernel(tc, query, key, value, attn_mask, out):
         nc.scalar.activation(out=warm[:, 1:2], in_=warm[:, 0:1], func=ACT.Tanh)
         bias_raw = sb.tile([P, NT, S], BF16, name="bias_raw", tag="bias_raw")
         b20 = sb.tile([P, NT, S], F32, name="b20", tag="b20")
-        load_keys(k_raw, k_rows, 0, "k_raw")
+        load_head(k_raw, k_rows, 0, "k_raw")
         load_head(q_raw, q_rows, 0, "q_raw")
         nc.sync.dma_start(out=bias_raw[:, 0:2, :], in_=bias_rows[:, 0:2, :])
         nc.sync.dma_start(out=bias_raw[:, 2:4, :], in_=bias_rows[:, 2:4, :])
-        load_keys(k_raw, k_rows, 1, "k_raw")
+        load_head(k_raw, k_rows, 1, "k_raw")
         load_head(q_raw, q_rows, 1, "q_raw")
         nc.sync.dma_start(out=bias_raw[:, 4:8, :], in_=bias_rows[:, 4:8, :])
         load_keys(v_raw, v_rows, 0, "v_raw")
         load_keys(v_raw, v_rows, 1, "v_raw")
         ident = sb.tile([P, P], BF16, name="ident", tag="ident")
         make_identity(nc, ident[:])
+        ident_f32 = sb.tile([P, P], F32, name="ident_f32", tag="ident_f32")
+        make_identity(nc, ident_f32[:])
         keep_head(k_t, transpose_head(k_raw[0]), 0, "k_t", nc.vector.tensor_copy)
         keep_head(q_t, transpose_head(q_raw[0]), 0, "q_t", nc.scalar.copy)
         scale_bias(0, nc.vector.tensor_scalar_mul)
@@ -317,6 +321,6 @@ def tile_naivesdpa_kernel(tc, query, key, value, attn_mask, out):
                 if part == 1:
                     waiting["q"] = transpose_head(q_raw[next_head])
             if part == 1 and h + 2 < H:
-                load_keys(k_raw, k_rows, h + 2, "k_raw")
+                load_head(k_raw, k_rows, h + 2, "k_raw")
                 load_head(q_raw, q_rows, h + 2, "q_raw")
                 load_keys(v_raw, v_rows, h + 2, "v_raw")

@@ -27,14 +27,15 @@ NBANK = 4 * NPAIR
 SOFT_CAP = 20.0
 FLOPS = 2 * 2 * H * S * S * D
 
-V_COLS = 320
-G_COLS = S - V_COLS
+TURNED_TILES = 2
+TURNED = TURNED_TILES * P
+PLAIN = S - TURNED
 
+TURN_LAG = 2
 MAX_LAG = 2
 EXP_LAG = 3
-COPY_LAG = 4
-QUANT_LAG = 5
-NORM_LAG = 6
+QUANT_LAG = 4
+NORM_LAG = 5
 
 SBUF_DEPTH = {
     "k_raw": 3,
@@ -45,20 +46,24 @@ SBUF_DEPTH = {
     "v_grouped": 2,
     "v_words": 3,
     "v_scales": 3,
-    "tanh_sb": 3,
+    "tanh_sb": TURN_LAG + 3,
     "capped": EXP_LAG + 1,
+    "plain_max": 2,
+    "turned_max": 2,
     "neg_max": 2,
     "exp_bias": 2,
     "e": 4,
-    "e_grouped": QUANT_LAG - EXP_LAG + 1,
+    "e_grouped": 3,
     "e_words": 2,
     "e_scales": 2,
-    "row_sum": NORM_LAG - EXP_LAG + 1,
+    "part_sum": QUANT_LAG - EXP_LAG + 2,
+    "row_sum": 2,
     "row_inv": 2,
     "out_sb": 2,
 }
 SCORE_BANKS = 3
-TRANSPOSE_BANKS = 4
+TURNED_BANKS = 2
+TRANSPOSE_BANKS = 2
 OUT_BANKS = 1
 
 
@@ -77,8 +82,8 @@ def tile_naivesdpa_kernel(tc, query, key, value, attn_mask, out):
         ctx.enter_context(tc.manual_schedule())
 
         k_raw, q_raw, v_raw, k_t, q_t, v_grouped, v_words, v_scales, out_sb = {}, {}, {}, {}, {}, {}, {}, {}, {}
-        scores, tanh_sb, capped, neg_max, exp_bias, e_t, e_grouped, e_words, e_scales = {}, {}, {}, {}, {}, {}, {}, {}, {}
-        row_sum, row_inv, out_ps = {}, {}, {}
+        scores, tanh_sb, capped, turned, exp_bias, e_sb, e_t, e_grouped, e_words, e_scales = {}, {}, {}, {}, {}, {}, {}, {}, {}, {}
+        plain_max, turned_max, neg_max, part_sum, row_sum, row_inv, out_ps, turned_bias_ps = {}, {}, {}, {}, {}, {}, {}, {}
 
         def sbuf(tag, shape, dtype):
             return sb.tile(shape, dtype, name=tag, tag=tag, bufs=SBUF_DEPTH[tag], align_bytes=64)
@@ -87,10 +92,10 @@ def tile_naivesdpa_kernel(tc, query, key, value, attn_mask, out):
             store[h] = sbuf(tag, [P, NT, D], BF16)
             nc.sync.dma_start(out=store[h][:], in_=rows[:, :, h, :])
 
-        def load_keys(store, rows, h, tag):
-            store[h] = sbuf(tag, [P, NT, D], BF16)
+        def load_v(h):
+            v_raw[h] = sbuf("v_raw", [P, NT, D], BF16)
             for g in range(PASSES):
-                nc.sync.dma_start(out=store[h][:, PACK * g:PACK * (g + 1), :], in_=rows[:, g, :, h, :])
+                nc.sync.dma_start(out=v_raw[h][:, PACK * g:PACK * (g + 1), :], in_=v_rows[:, g, :, h, :])
 
         def transpose_head(raw):
             bank = ps.tile([P, S], BF16, name="head_t", tag="t", bufs=TRANSPOSE_BANKS)
@@ -114,22 +119,41 @@ def tile_naivesdpa_kernel(tc, query, key, value, attn_mask, out):
             v_scales[h] = sbuf("v_scales", [P, PASSES * D], U8)
             nc.vector.quantize_mx(out=v_words[h][:].bitcast(FP8X4), scales=v_scales[h][:], in_=v_grouped[h][:])
 
-        def scale_bias(j, mul):
-            mul(b20[:, j, :], bias_raw[:, j, :], 1.0 / SOFT_CAP)
+        def scale_plain_bias(j, mul):
+            mul(b20[:, j, :], bias_raw[:, j, 0:PLAIN], 1.0 / SOFT_CAP)
+
+        def turn_bias(pair):
+            bank = ps.tile([P, TURNED_TILES, 2 * P], BF16, name="bias_turn", tag="t", bufs=TRANSPOSE_BANKS)
+            for u in range(2):
+                for i in range(TURNED_TILES):
+                    nc.tensor.transpose(
+                        bank[:, i, u * P:(u + 1) * P], bias_raw[:, 2 * pair + u, PLAIN + i * P:PLAIN + (i + 1) * P], ident[:]
+                    )
+            turned_bias_ps[pair] = bank
+
+        def scale_turned_bias(pair):
+            nc.vector.tensor_scalar_mul(bias_t[:, :, 2 * P * pair:2 * P * (pair + 1)], turned_bias_ps[pair][:], 1.0 / SOFT_CAP)
 
         def score_bank(x):
             pair, b = divmod(x, 4)
             h = pair // PAIRS_PER_HEAD
             tile_no = 2 * (pair % PAIRS_PER_HEAD) + b // 2
-            half = b % 2
+            q_tile = q_t[h][:, tile_no * P:(tile_no + 1) * P]
             scores[x] = ps.tile([P, BANK], F32, name="scores", tag="scores", bufs=SCORE_BANKS)
-            nc.tensor.matmul(
-                scores[x][:],
-                lhsT=q_t[h][:, tile_no * P:(tile_no + 1) * P],
-                rhs=k_t[h][:, half * BANK:(half + 1) * BANK],
-                start=True,
-                stop=True,
-            )
+            if b % 2 == 0:
+                nc.tensor.matmul(scores[x][:], lhsT=q_tile, rhs=k_t[h][:, 0:BANK], start=True, stop=True)
+            else:
+                nc.tensor.matmul(
+                    scores[x][:, 0:PLAIN - BANK], lhsT=q_tile, rhs=k_t[h][:, BANK:PLAIN], start=True, stop=True
+                )
+                for i in range(TURNED_TILES):
+                    nc.tensor.matmul(
+                        scores[x][:, PLAIN - BANK + i * P:PLAIN - BANK + (i + 1) * P],
+                        lhsT=k_t[h][:, PLAIN + i * P:PLAIN + (i + 1) * P],
+                        rhs=q_tile,
+                        start=True,
+                        stop=True,
+                    )
 
         def tanh_bank(x):
             pair, b = divmod(x, 4)
@@ -140,17 +164,33 @@ def tile_naivesdpa_kernel(tc, query, key, value, attn_mask, out):
             if x + SCORE_BANKS < NBANK:
                 score_bank(x + SCORE_BANKS)
 
-        def add_bias(pair, engine, cols):
+        def add_plain_bias(pair):
             j = 2 * (pair % PAIRS_PER_HEAD)
-            engine.tensor_tensor(
-                out=capped[pair][:, :, cols], in0=tanh_sb[pair][:, :, cols], in1=b20[:, j:j + 2, cols], op=ALU.add
+            capped[pair] = sbuf("capped", [P, 2, PLAIN], F32)
+            nc.gpsimd.tensor_tensor(
+                out=capped[pair][:], in0=tanh_sb[pair][:, :, 0:PLAIN], in1=b20[:, j:j + 2, :], op=ALU.add
             )
 
-        def row_max(pair):
-            neg_max[pair] = sbuf("neg_max", [P, 2], F32)
+        def add_turned_bias(pair, u):
+            if u == 0:
+                turned[pair] = ps.tile([P, 2, TURNED], F32, name="turned", tag="turned", bufs=TURNED_BANKS)
+            tile_no = 2 * (pair % PAIRS_PER_HEAD) + u
+            for i in range(TURNED_TILES):
+                total = turned[pair][:, u, i * P:(i + 1) * P]
+                bias_tile = bias_t[:, i, tile_no * P:(tile_no + 1) * P]
+                tanh_tile = tanh_sb[pair][:, u, PLAIN + i * P:PLAIN + (i + 1) * P]
+                nc.tensor.matmul(total, lhsT=bias_tile, rhs=ident_f32[:], is_transpose=True, start=True, stop=False)
+                nc.tensor.matmul(total, lhsT=tanh_tile, rhs=ident_f32[:], is_transpose=True, start=False, stop=True)
+
+        def max_of(store, pair, source, tag):
+            store[pair] = sbuf(tag, [P, 2], F32)
             nc.vector.tensor_reduce(
-                out=neg_max[pair][:], in_=capped[pair][:], axis=mybir.AxisListType.X, op=ALU.max, negate=True
+                out=store[pair][:], in_=source[pair][:], axis=mybir.AxisListType.X, op=ALU.max, negate=True
             )
+
+        def join_max(pair):
+            neg_max[pair] = sbuf("neg_max", [P, 2], F32)
+            nc.vector.tensor_tensor(out=neg_max[pair][:], in0=plain_max[pair][:], in1=turned_max[pair][:], op=ALU.min)
 
         def scale_max(pair):
             exp_bias[pair] = sbuf("exp_bias", [P, 2], F32)
@@ -160,18 +200,21 @@ def tile_naivesdpa_kernel(tc, query, key, value, attn_mask, out):
 
         def exp_unit(pair, u):
             if u == 0:
-                row_sum[pair] = sbuf("row_sum", [P, 2], F32)
-            e = sbuf("e", [P, S], BF16)
-            nc.scalar.activation(
-                out=e[:],
-                in_=capped[pair][:, u, :],
-                func=ACT.Exp,
-                bias=exp_bias[pair][:, u:u + 1],
-                scale=SOFT_CAP,
-                accum_out=row_sum[pair][:, u:u + 1],
-            )
+                part_sum[pair] = sbuf("part_sum", [P, 2, 2], F32)
+            e_sb[(pair, u)] = sbuf("e", [P, S], BF16)
+            for part, (cols, source) in enumerate(((slice(0, PLAIN), capped), (slice(PLAIN, S), turned))):
+                nc.scalar.activation(
+                    out=e_sb[(pair, u)][:, cols],
+                    in_=source[pair][:, u, :],
+                    func=ACT.Exp,
+                    bias=exp_bias[pair][:, u:u + 1],
+                    scale=SOFT_CAP,
+                    accum_out=part_sum[pair][:, u, part:part + 1],
+                )
+
+        def transpose_e(pair, u):
             e_t[(pair, u)] = ps.tile([P, WORDS], F32, name="e_t", tag="t", bufs=TRANSPOSE_BANKS)
-            words = e[:].bitcast(F32)
+            words = e_sb[(pair, u)][:].bitcast(F32)
             for g in range(PASSES):
                 for i in range(2):
                     block = 2 * g + i
@@ -179,10 +222,10 @@ def tile_naivesdpa_kernel(tc, query, key, value, attn_mask, out):
                         e_t[(pair, u)][:, block * P:(block + 1) * P], words[:, 2 * P * g + i:2 * P * (g + 1):2], ident_f32[:]
                     )
 
-        def group_e(pair, u, copy):
+        def group_e(pair, u):
             if u == 0:
                 e_grouped[pair] = sbuf("e_grouped", [P, 2, S], BF16)
-            copy(
+            nc.vector.tensor_copy(
                 out=e_grouped[pair][:, u, :].bitcast(F32).rearrange("p (g q i) -> p g q i", g=PASSES, i=2),
                 in_=e_t[(pair, u)][:].rearrange("p (g i q) -> p g q i", g=PASSES, i=2),
             )
@@ -213,6 +256,12 @@ def tile_naivesdpa_kernel(tc, query, key, value, attn_mask, out):
                         stop=(g == PASSES - 1),
                     )
 
+        def join_sum(pair):
+            row_sum[pair] = sbuf("row_sum", [P, 2], F32)
+            nc.gpsimd.tensor_tensor(
+                out=row_sum[pair][:], in0=part_sum[pair][:, :, 0], in1=part_sum[pair][:, :, 1], op=ALU.add
+            )
+
         def invert_sum(pair):
             row_inv[pair] = sbuf("row_inv", [P, 2], F32)
             nc.vector.reciprocal(row_inv[pair][:], row_sum[pair][:])
@@ -237,7 +286,8 @@ def tile_naivesdpa_kernel(tc, query, key, value, attn_mask, out):
         nc.vector.memset(warm[:, 0:1], 0.0)
         nc.scalar.activation(out=warm[:, 1:2], in_=warm[:, 0:1], func=ACT.Tanh)
         bias_raw = sb.tile([P, NT, S], BF16, name="bias_raw", tag="bias_raw")
-        b20 = sb.tile([P, NT, S], F32, name="b20", tag="b20")
+        b20 = sb.tile([P, NT, PLAIN], F32, name="b20", tag="b20")
+        bias_t = sb.tile([P, TURNED_TILES, S], F32, name="bias_t", tag="bias_t")
         load_head(k_raw, k_rows, 0, "k_raw")
         load_head(q_raw, q_rows, 0, "q_raw")
         nc.sync.dma_start(out=bias_raw[:, 0:2, :], in_=bias_rows[:, 0:2, :])
@@ -245,19 +295,18 @@ def tile_naivesdpa_kernel(tc, query, key, value, attn_mask, out):
         load_head(k_raw, k_rows, 1, "k_raw")
         load_head(q_raw, q_rows, 1, "q_raw")
         nc.sync.dma_start(out=bias_raw[:, 4:8, :], in_=bias_rows[:, 4:8, :])
-        load_keys(v_raw, v_rows, 0, "v_raw")
-        load_keys(v_raw, v_rows, 1, "v_raw")
+        load_v(0)
+        load_v(1)
         ident = sb.tile([P, P], BF16, name="ident", tag="ident")
         make_identity(nc, ident[:])
         ident_f32 = sb.tile([P, P], F32, name="ident_f32", tag="ident_f32")
         make_identity(nc, ident_f32[:])
         keep_head(k_t, transpose_head(k_raw[0]), 0, "k_t", nc.vector.tensor_copy)
         keep_head(q_t, transpose_head(q_raw[0]), 0, "q_t", nc.scalar.copy)
-        scale_bias(0, nc.vector.tensor_scalar_mul)
-        scale_bias(1, nc.vector.tensor_scalar_mul)
         for x in range(SCORE_BANKS):
             score_bank(x)
-        waiting = {}
+        scale_plain_bias(0, nc.vector.tensor_scalar_mul)
+        scale_plain_bias(1, nc.vector.tensor_scalar_mul)
 
         for n in range(NPAIR + NORM_LAG + 1):
             h, part = divmod(n, PAIRS_PER_HEAD)
@@ -267,27 +316,44 @@ def tile_naivesdpa_kernel(tc, query, key, value, attn_mask, out):
                 tanh_sb[n] = sbuf("tanh_sb", [P, 2, S], F32)
                 tanh_bank(4 * n)
                 tanh_bank(4 * n + 1)
-            if live(n - EXP_LAG):
-                exp_unit(n - EXP_LAG, 0)
+            new_k = next_head is not None and part == 1
+            new_q = next_head is not None and part == 2
+            if new_k:
+                head_bank = transpose_head(k_raw[next_head])
+            if new_q:
+                head_bank = transpose_head(q_raw[next_head])
             if live(n):
                 tanh_bank(4 * n + 2)
                 tanh_bank(4 * n + 3)
+            if live(n - TURN_LAG):
+                add_turned_bias(n - TURN_LAG, 0)
+                add_turned_bias(n - TURN_LAG, 1)
             if 1 <= n < PAIRS_PER_HEAD:
-                scale_bias(2 * n, nc.scalar.mul)
-                scale_bias(2 * n + 1, nc.scalar.mul)
+                scale_plain_bias(2 * n, nc.scalar.mul)
+                scale_plain_bias(2 * n + 1, nc.scalar.mul)
+            if live(n - NORM_LAG):
+                e_times_v(n - NORM_LAG)
+            if live(n - EXP_LAG):
+                exp_unit(n - EXP_LAG, 0)
+            if new_k:
+                keep_head(k_t, head_bank, next_head, "k_t", nc.scalar.copy)
+            if live(n - EXP_LAG):
+                transpose_e(n - EXP_LAG, 0)
+            if new_q:
+                keep_head(q_t, head_bank, next_head, "q_t", nc.vector.tensor_copy)
             if live(n - EXP_LAG):
                 exp_unit(n - EXP_LAG, 1)
-                group_e(n - EXP_LAG, 0, nc.scalar.copy)
+                transpose_e(n - EXP_LAG, 1)
 
             if live(n - MAX_LAG):
-                row_max(n - MAX_LAG)
+                max_of(plain_max, n - MAX_LAG, capped, "plain_max")
+                max_of(turned_max, n - MAX_LAG, turned, "turned_max")
             if live(n - QUANT_LAG):
                 quantise_e(n - QUANT_LAG)
+            if live(n - MAX_LAG):
+                join_max(n - MAX_LAG)
             if live(n - NORM_LAG):
                 invert_sum(n - NORM_LAG)
-            if live(n):
-                capped[n] = sbuf("capped", [P, 2, S], F32)
-                add_bias(n, nc.vector, slice(G_COLS, S))
             if part == 2:
                 if h == 0:
                     group_v(0)
@@ -302,25 +368,20 @@ def tile_naivesdpa_kernel(tc, query, key, value, attn_mask, out):
             if live(n - MAX_LAG):
                 scale_max(n - MAX_LAG)
             if live(n):
-                add_bias(n, nc.gpsimd, slice(0, G_COLS))
+                add_plain_bias(n)
+            if live(n - QUANT_LAG):
+                join_sum(n - QUANT_LAG)
 
+            if live(n - EXP_LAG):
+                group_e(n - EXP_LAG, 0)
             if live(n - NORM_LAG):
                 divide_and_store(n - NORM_LAG)
-            if live(n - QUANT_LAG):
-                e_times_v(n - QUANT_LAG)
-            if live(n - COPY_LAG):
-                group_e(n - COPY_LAG, 1, nc.vector.tensor_copy)
-
-            if next_head is not None:
-                if part == 1:
-                    keep_head(k_t, waiting["k"], next_head, "k_t", nc.vector.tensor_copy)
-                if part == 2:
-                    keep_head(q_t, waiting["q"], next_head, "q_t", nc.vector.tensor_copy)
-                if part == 0:
-                    waiting["k"] = transpose_head(k_raw[next_head])
-                if part == 1:
-                    waiting["q"] = transpose_head(q_raw[next_head])
-            if part == 1 and h + 2 < H:
+            if live(n - EXP_LAG):
+                group_e(n - EXP_LAG, 1)
+            if n < PAIRS_PER_HEAD:
+                turn_bias(n)
+                scale_turned_bias(n)
+            if part == 2 and h + 2 < H:
                 load_head(k_raw, k_rows, h + 2, "k_raw")
                 load_head(q_raw, q_rows, h + 2, "q_raw")
-                load_keys(v_raw, v_rows, h + 2, "v_raw")
+                load_v(h + 2)

@@ -83,7 +83,7 @@ def tile_naivesdpa_kernel(tc, query, key, value, attn_mask, out):
 
         k_raw, q_raw, v_raw, k_t, q_t, v_grouped, v_words, v_scales, out_sb = {}, {}, {}, {}, {}, {}, {}, {}, {}
         scores, tanh_sb, capped, turned, exp_bias, e_sb, e_t, e_grouped, e_words, e_scales = {}, {}, {}, {}, {}, {}, {}, {}, {}, {}
-        plain_max, turned_max, neg_max, part_sum, row_sum, row_inv, out_ps, turned_bias_ps = {}, {}, {}, {}, {}, {}, {}, {}
+        plain_max, turned_max, neg_max, part_sum, row_sum, row_inv, out_ps = {}, {}, {}, {}, {}, {}, {}
 
         def sbuf(tag, shape, dtype):
             return sb.tile(shape, dtype, name=tag, tag=tag, bufs=SBUF_DEPTH[tag], align_bytes=64)
@@ -103,9 +103,16 @@ def tile_naivesdpa_kernel(tc, query, key, value, attn_mask, out):
                 nc.tensor.transpose(bank[:, j * P:(j + 1) * P], raw[:, j, :], ident[:])
             return bank
 
-        def keep_head(store, bank, h, tag, copy):
-            store[h] = sbuf(tag, [P, S], BF16)
-            copy(out=store[h][:], in_=bank[:])
+        def keep_q(h, bank, copy):
+            q_t[h] = sbuf("q_t", [P, S], BF16)
+            copy(out=q_t[h][:], in_=bank[:])
+
+        def keep_k(h, bank, copy):
+            k_t[h] = sbuf("k_t", [P, S], BF16)
+            copy(
+                out=k_t[h][:].bitcast(F32).rearrange("d (g i p) -> d g i p", g=PASSES, i=2),
+                in_=bank[:].bitcast(F32).rearrange("d (g p i) -> d g i p", g=PASSES, i=2),
+            )
 
         def group_v(h):
             v_grouped[h] = sbuf("v_grouped", [P, S], BF16)
@@ -119,20 +126,23 @@ def tile_naivesdpa_kernel(tc, query, key, value, attn_mask, out):
             v_scales[h] = sbuf("v_scales", [P, PASSES * D], U8)
             nc.vector.quantize_mx(out=v_words[h][:].bitcast(FP8X4), scales=v_scales[h][:], in_=v_grouped[h][:])
 
-        def scale_plain_bias(j, mul):
-            mul(b20[:, j, :], bias_raw[:, j, 0:PLAIN], 1.0 / SOFT_CAP)
+        def scale_bias(j, mul):
+            for g in range(PASSES):
+                cols = slice(g * BANK, (g + 1) * BANK)
+                mul(
+                    b20[:, j, cols].rearrange("q (i p c) -> q i p c", i=2, c=2),
+                    bias_raw[:, j, cols].rearrange("q (p i c) -> q i p c", i=2, c=2),
+                    1.0 / SOFT_CAP,
+                )
 
         def turn_bias(pair):
-            bank = ps.tile([P, TURNED_TILES, 2 * P], BF16, name="bias_turn", tag="t", bufs=TRANSPOSE_BANKS)
+            bank = ps.tile([P, TURNED_TILES, 2 * P], F32, name="bias_turn", tag="t", bufs=TRANSPOSE_BANKS)
             for u in range(2):
                 for i in range(TURNED_TILES):
                     nc.tensor.transpose(
-                        bank[:, i, u * P:(u + 1) * P], bias_raw[:, 2 * pair + u, PLAIN + i * P:PLAIN + (i + 1) * P], ident[:]
+                        bank[:, i, u * P:(u + 1) * P], b20[:, 2 * pair + u, PLAIN + i * P:PLAIN + (i + 1) * P], ident_f32[:]
                     )
-            turned_bias_ps[pair] = bank
-
-        def scale_turned_bias(pair):
-            nc.vector.tensor_scalar_mul(bias_t[:, :, 2 * P * pair:2 * P * (pair + 1)], turned_bias_ps[pair][:], 1.0 / SOFT_CAP)
+            nc.vector.tensor_copy(out=bias_t[:, :, 2 * P * pair:2 * P * (pair + 1)], in_=bank[:])
 
         def score_bank(x):
             pair, b = divmod(x, 4)
@@ -168,7 +178,7 @@ def tile_naivesdpa_kernel(tc, query, key, value, attn_mask, out):
             j = 2 * (pair % PAIRS_PER_HEAD)
             capped[pair] = sbuf("capped", [P, 2, PLAIN], F32)
             nc.gpsimd.tensor_tensor(
-                out=capped[pair][:], in0=tanh_sb[pair][:, :, 0:PLAIN], in1=b20[:, j:j + 2, :], op=ALU.add
+                out=capped[pair][:], in0=tanh_sb[pair][:, :, 0:PLAIN], in1=b20[:, j:j + 2, 0:PLAIN], op=ALU.add
             )
 
         def add_turned_bias(pair, u):
@@ -215,12 +225,9 @@ def tile_naivesdpa_kernel(tc, query, key, value, attn_mask, out):
         def transpose_e(pair, u):
             e_t[(pair, u)] = ps.tile([P, WORDS], F32, name="e_t", tag="t", bufs=TRANSPOSE_BANKS)
             words = e_sb[(pair, u)][:].bitcast(F32)
-            for g in range(PASSES):
-                for i in range(2):
-                    block = 2 * g + i
-                    nc.tensor.transpose(
-                        e_t[(pair, u)][:, block * P:(block + 1) * P], words[:, 2 * P * g + i:2 * P * (g + 1):2], ident_f32[:]
-                    )
+            for block in range(WORDS // P):
+                cols = slice(block * P, (block + 1) * P)
+                nc.tensor.transpose(e_t[(pair, u)][:, cols], words[:, cols], ident_f32[:])
 
         def group_e(pair, u):
             if u == 0:
@@ -286,7 +293,7 @@ def tile_naivesdpa_kernel(tc, query, key, value, attn_mask, out):
         nc.vector.memset(warm[:, 0:1], 0.0)
         nc.scalar.activation(out=warm[:, 1:2], in_=warm[:, 0:1], func=ACT.Tanh)
         bias_raw = sb.tile([P, NT, S], BF16, name="bias_raw", tag="bias_raw")
-        b20 = sb.tile([P, NT, PLAIN], F32, name="b20", tag="b20")
+        b20 = sb.tile([P, NT, S], F32, name="b20", tag="b20")
         bias_t = sb.tile([P, TURNED_TILES, S], F32, name="bias_t", tag="bias_t")
         load_head(k_raw, k_rows, 0, "k_raw")
         load_head(q_raw, q_rows, 0, "q_raw")
@@ -301,12 +308,12 @@ def tile_naivesdpa_kernel(tc, query, key, value, attn_mask, out):
         make_identity(nc, ident[:])
         ident_f32 = sb.tile([P, P], F32, name="ident_f32", tag="ident_f32")
         make_identity(nc, ident_f32[:])
-        keep_head(k_t, transpose_head(k_raw[0]), 0, "k_t", nc.vector.tensor_copy)
-        keep_head(q_t, transpose_head(q_raw[0]), 0, "q_t", nc.scalar.copy)
+        keep_k(0, transpose_head(k_raw[0]), nc.vector.tensor_copy)
+        keep_q(0, transpose_head(q_raw[0]), nc.scalar.copy)
         for x in range(SCORE_BANKS):
             score_bank(x)
-        scale_plain_bias(0, nc.vector.tensor_scalar_mul)
-        scale_plain_bias(1, nc.vector.tensor_scalar_mul)
+        scale_bias(0, nc.vector.tensor_scalar_mul)
+        scale_bias(1, nc.vector.tensor_scalar_mul)
 
         for n in range(NPAIR + NORM_LAG + 1):
             h, part = divmod(n, PAIRS_PER_HEAD)
@@ -329,18 +336,18 @@ def tile_naivesdpa_kernel(tc, query, key, value, attn_mask, out):
                 add_turned_bias(n - TURN_LAG, 0)
                 add_turned_bias(n - TURN_LAG, 1)
             if 1 <= n < PAIRS_PER_HEAD:
-                scale_plain_bias(2 * n, nc.scalar.mul)
-                scale_plain_bias(2 * n + 1, nc.scalar.mul)
+                scale_bias(2 * n, nc.scalar.mul)
+                scale_bias(2 * n + 1, nc.scalar.mul)
             if live(n - NORM_LAG):
                 e_times_v(n - NORM_LAG)
             if live(n - EXP_LAG):
                 exp_unit(n - EXP_LAG, 0)
             if new_k:
-                keep_head(k_t, head_bank, next_head, "k_t", nc.scalar.copy)
+                keep_k(next_head, head_bank, nc.scalar.copy)
             if live(n - EXP_LAG):
                 transpose_e(n - EXP_LAG, 0)
             if new_q:
-                keep_head(q_t, head_bank, next_head, "q_t", nc.vector.tensor_copy)
+                keep_q(next_head, head_bank, nc.vector.tensor_copy)
             if live(n - EXP_LAG):
                 exp_unit(n - EXP_LAG, 1)
                 transpose_e(n - EXP_LAG, 1)
@@ -380,7 +387,6 @@ def tile_naivesdpa_kernel(tc, query, key, value, attn_mask, out):
                 group_e(n - EXP_LAG, 1)
             if n < PAIRS_PER_HEAD:
                 turn_bias(n)
-                scale_turned_bias(n)
             if part == 2 and h + 2 < H:
                 load_head(k_raw, k_rows, h + 2, "k_raw")
                 load_head(q_raw, q_rows, h + 2, "q_raw")

@@ -50,7 +50,6 @@ SBUF_DEPTH = {
     "capped": EXP_LAG + 1,
     "plain_max": 2,
     "turned_max": 2,
-    "neg_max": 2,
     "exp_bias": 2,
     "e": 4,
     "e_grouped": 3,
@@ -75,6 +74,7 @@ def tile_naivesdpa_kernel(tc, query, key, value, attn_mask, out):
     bias_rows = attn_mask.rearrange("a b (j p) k -> p (a b j) k", p=P)
     out_rows = out.rearrange("b (j p) h d -> p (b j) h d", p=P)
     tanh_scale = 1.0 / (math.sqrt(D) * SOFT_CAP)
+    all_tiles = slice(0, NT)
 
     with ExitStack() as ctx:
         sb = ctx.enter_context(tc.tile_pool(name="sb", bufs=1))
@@ -88,30 +88,35 @@ def tile_naivesdpa_kernel(tc, query, key, value, attn_mask, out):
         def sbuf(tag, shape, dtype):
             return sb.tile(shape, dtype, name=tag, tag=tag, bufs=SBUF_DEPTH[tag], align_bytes=64)
 
-        def load_head(store, rows, h, tag):
-            store[h] = sbuf(tag, [P, NT, D], BF16)
-            nc.sync.dma_start(out=store[h][:], in_=rows[:, :, h, :])
+        def load_tiles(store, rows, h, tag, tiles):
+            if tiles.start == 0:
+                store[h] = sbuf(tag, [P, NT, D], BF16)
+            nc.sync.dma_start(out=store[h][:, tiles, :], in_=rows[:, tiles, h, :])
 
         def load_v(h):
             v_raw[h] = sbuf("v_raw", [P, NT, D], BF16)
             for g in range(PASSES):
                 nc.sync.dma_start(out=v_raw[h][:, PACK * g:PACK * (g + 1), :], in_=v_rows[:, g, :, h, :])
 
-        def transpose_head(raw):
-            bank = ps.tile([P, S], BF16, name="head_t", tag="t", bufs=TRANSPOSE_BANKS)
-            for j in range(NT):
-                nc.tensor.transpose(bank[:, j * P:(j + 1) * P], raw[:, j, :], ident[:])
+        def transpose_tiles(raw, tiles):
+            count = tiles.stop - tiles.start
+            bank = ps.tile([P, count * P], BF16, name="head_t", tag="t", bufs=TRANSPOSE_BANKS)
+            for j in range(count):
+                nc.tensor.transpose(bank[:, j * P:(j + 1) * P], raw[:, tiles.start + j, :], ident[:])
             return bank
 
-        def keep_q(h, bank, copy):
-            q_t[h] = sbuf("q_t", [P, S], BF16)
-            copy(out=q_t[h][:], in_=bank[:])
+        def keep_q(h, bank, copy, tiles):
+            if tiles.start == 0:
+                q_t[h] = sbuf("q_t", [P, S], BF16)
+            copy(out=q_t[h][:, tiles.start * P:tiles.stop * P].bitcast(F32), in_=bank[:].bitcast(F32))
 
-        def keep_k(h, bank, copy):
-            k_t[h] = sbuf("k_t", [P, S], BF16)
+        def keep_k(h, bank, copy, tiles):
+            if tiles.start == 0:
+                k_t[h] = sbuf("k_t", [P, S], BF16)
+            passes = (tiles.stop - tiles.start) // PACK
             copy(
-                out=k_t[h][:].bitcast(F32).rearrange("d (g i p) -> d g i p", g=PASSES, i=2),
-                in_=bank[:].bitcast(F32).rearrange("d (g p i) -> d g i p", g=PASSES, i=2),
+                out=k_t[h][:, tiles.start * P:tiles.stop * P].bitcast(F32).rearrange("d (g i p) -> d g i p", g=passes, i=2),
+                in_=bank[:].bitcast(F32).rearrange("d (g p i) -> d g i p", g=passes, i=2),
             )
 
         def group_v(h):
@@ -176,7 +181,6 @@ def tile_naivesdpa_kernel(tc, query, key, value, attn_mask, out):
 
         def add_plain_bias(pair):
             j = 2 * (pair % PAIRS_PER_HEAD)
-            capped[pair] = sbuf("capped", [P, 2, PLAIN], F32)
             nc.gpsimd.tensor_tensor(
                 out=capped[pair][:], in0=tanh_sb[pair][:, :, 0:PLAIN], in1=b20[:, j:j + 2, 0:PLAIN], op=ALU.add
             )
@@ -193,34 +197,32 @@ def tile_naivesdpa_kernel(tc, query, key, value, attn_mask, out):
                 nc.tensor.matmul(total, lhsT=tanh_tile, rhs=ident_f32[:], is_transpose=True, start=False, stop=True)
 
         def max_of(store, pair, source, tag):
-            store[pair] = sbuf(tag, [P, 2], F32)
+            store[pair] = sbuf(tag, [P, 2, 1], F32)
             nc.vector.tensor_reduce(
-                out=store[pair][:], in_=source[pair][:], axis=mybir.AxisListType.X, op=ALU.max, negate=True
+                out=store[pair][:, :, 0], in_=source[pair][:], axis=mybir.AxisListType.X, op=ALU.max, negate=True
             )
 
-        def join_max(pair):
-            neg_max[pair] = sbuf("neg_max", [P, 2], F32)
-            nc.vector.tensor_tensor(out=neg_max[pair][:], in0=plain_max[pair][:], in1=turned_max[pair][:], op=ALU.min)
+        def join_max(pair, host):
+            neg_max[pair] = host[:, :, 0:1]
+            nc.vector.tensor_tensor(out=neg_max[pair], in0=plain_max[pair][:], in1=turned_max[pair][:], op=ALU.min)
 
         def scale_max(pair):
-            exp_bias[pair] = sbuf("exp_bias", [P, 2], F32)
-            nc.gpsimd.tensor_scalar(
-                out=exp_bias[pair][:], in0=neg_max[pair][:], scalar1=SOFT_CAP, scalar2=0.0, op0=ALU.mult, op1=ALU.add
-            )
+            exp_bias[pair] = sbuf("exp_bias", [P, 2, 1], F32)
+            nc.vector.tensor_scalar_mul(exp_bias[pair][:], neg_max[pair], SOFT_CAP)
 
-        def exp_unit(pair, u):
-            if u == 0:
-                part_sum[pair] = sbuf("part_sum", [P, 2, 2], F32)
-            e_sb[(pair, u)] = sbuf("e", [P, S], BF16)
-            for part, (cols, source) in enumerate(((slice(0, PLAIN), capped), (slice(PLAIN, S), turned))):
-                nc.scalar.activation(
-                    out=e_sb[(pair, u)][:, cols],
-                    in_=source[pair][:, u, :],
-                    func=ACT.Exp,
-                    bias=exp_bias[pair][:, u:u + 1],
-                    scale=SOFT_CAP,
-                    accum_out=part_sum[pair][:, u, part:part + 1],
-                )
+        def exp_keys(pair, u, part):
+            if part == 0:
+                if u == 0:
+                    part_sum[pair] = sbuf("part_sum", [P, 2, 2], F32)
+                e_sb[(pair, u)] = sbuf("e", [P, S], BF16)
+            nc.scalar.activation(
+                out=e_sb[(pair, u)][:, slice(0, PLAIN) if part == 0 else slice(PLAIN, S)],
+                in_=(capped if part == 0 else turned)[pair][:, u, :],
+                func=ACT.Exp,
+                bias=exp_bias[pair][:, u, :],
+                scale=SOFT_CAP,
+                accum_out=part_sum[pair][:, u, part:part + 1],
+            )
 
         def transpose_e(pair, u):
             e_t[(pair, u)] = ps.tile([P, WORDS], F32, name="e_t", tag="t", bufs=TRANSPOSE_BANKS)
@@ -229,10 +231,10 @@ def tile_naivesdpa_kernel(tc, query, key, value, attn_mask, out):
                 cols = slice(block * P, (block + 1) * P)
                 nc.tensor.transpose(e_t[(pair, u)][:, cols], words[:, cols], ident_f32[:])
 
-        def group_e(pair, u):
+        def group_e(pair, u, copy):
             if u == 0:
                 e_grouped[pair] = sbuf("e_grouped", [P, 2, S], BF16)
-            nc.vector.tensor_copy(
+            copy(
                 out=e_grouped[pair][:, u, :].bitcast(F32).rearrange("p (g q i) -> p g q i", g=PASSES, i=2),
                 in_=e_t[(pair, u)][:].rearrange("p (g i q) -> p g q i", g=PASSES, i=2),
             )
@@ -295,12 +297,16 @@ def tile_naivesdpa_kernel(tc, query, key, value, attn_mask, out):
         bias_raw = sb.tile([P, NT, S], BF16, name="bias_raw", tag="bias_raw")
         b20 = sb.tile([P, NT, S], F32, name="b20", tag="b20")
         bias_t = sb.tile([P, TURNED_TILES, S], F32, name="bias_t", tag="bias_t")
-        load_head(k_raw, k_rows, 0, "k_raw")
-        load_head(q_raw, q_rows, 0, "q_raw")
+        k_first, k_rest = slice(0, PACK), slice(PACK, NT)
+        q_first, q_rest = slice(0, 2), slice(2, NT)
+        load_tiles(k_raw, k_rows, 0, "k_raw", k_first)
+        load_tiles(q_raw, q_rows, 0, "q_raw", q_first)
+        load_tiles(k_raw, k_rows, 0, "k_raw", k_rest)
         nc.sync.dma_start(out=bias_raw[:, 0:2, :], in_=bias_rows[:, 0:2, :])
+        load_tiles(q_raw, q_rows, 0, "q_raw", q_rest)
         nc.sync.dma_start(out=bias_raw[:, 2:4, :], in_=bias_rows[:, 2:4, :])
-        load_head(k_raw, k_rows, 1, "k_raw")
-        load_head(q_raw, q_rows, 1, "q_raw")
+        load_tiles(k_raw, k_rows, 1, "k_raw", all_tiles)
+        load_tiles(q_raw, q_rows, 1, "q_raw", all_tiles)
         nc.sync.dma_start(out=bias_raw[:, 4:8, :], in_=bias_rows[:, 4:8, :])
         load_v(0)
         load_v(1)
@@ -308,10 +314,14 @@ def tile_naivesdpa_kernel(tc, query, key, value, attn_mask, out):
         make_identity(nc, ident[:])
         ident_f32 = sb.tile([P, P], F32, name="ident_f32", tag="ident_f32")
         make_identity(nc, ident_f32[:])
-        keep_k(0, transpose_head(k_raw[0]), nc.vector.tensor_copy)
-        keep_q(0, transpose_head(q_raw[0]), nc.scalar.copy)
-        for x in range(SCORE_BANKS):
+        k_bank, q_bank = transpose_tiles(k_raw[0], k_first), transpose_tiles(q_raw[0], q_first)
+        keep_k(0, k_bank, nc.vector.tensor_copy, k_first)
+        keep_q(0, q_bank, nc.scalar.copy, q_first)
+        score_bank(0)
+        keep_k(0, transpose_tiles(k_raw[0], k_rest), nc.vector.tensor_copy, k_rest)
+        for x in range(1, SCORE_BANKS):
             score_bank(x)
+        keep_q(0, transpose_tiles(q_raw[0], q_rest), nc.vector.tensor_copy, q_rest)
         scale_bias(0, nc.vector.tensor_scalar_mul)
         scale_bias(1, nc.vector.tensor_scalar_mul)
 
@@ -326,9 +336,9 @@ def tile_naivesdpa_kernel(tc, query, key, value, attn_mask, out):
             new_k = next_head is not None and part == 1
             new_q = next_head is not None and part == 2
             if new_k:
-                head_bank = transpose_head(k_raw[next_head])
+                head_bank = transpose_tiles(k_raw[next_head], all_tiles)
             if new_q:
-                head_bank = transpose_head(q_raw[next_head])
+                head_bank = transpose_tiles(q_raw[next_head], all_tiles)
             if live(n):
                 tanh_bank(4 * n + 2)
                 tanh_bank(4 * n + 3)
@@ -341,26 +351,34 @@ def tile_naivesdpa_kernel(tc, query, key, value, attn_mask, out):
             if live(n - NORM_LAG):
                 e_times_v(n - NORM_LAG)
             if live(n - EXP_LAG):
-                exp_unit(n - EXP_LAG, 0)
+                exp_keys(n - EXP_LAG, 0, 0)
             if new_k:
-                keep_k(next_head, head_bank, nc.scalar.copy)
-            if live(n - EXP_LAG):
-                transpose_e(n - EXP_LAG, 0)
+                keep_k(next_head, head_bank, nc.scalar.copy, all_tiles)
             if new_q:
-                keep_q(next_head, head_bank, nc.vector.tensor_copy)
+                keep_q(next_head, head_bank, nc.scalar.copy, all_tiles)
             if live(n - EXP_LAG):
-                exp_unit(n - EXP_LAG, 1)
+                exp_keys(n - EXP_LAG, 0, 1)
+                transpose_e(n - EXP_LAG, 0)
+                exp_keys(n - EXP_LAG, 1, 0)
+                exp_keys(n - EXP_LAG, 1, 1)
                 transpose_e(n - EXP_LAG, 1)
+            if live(n - EXP_LAG) and not live(n + 1):
+                group_e(n - EXP_LAG, 0, nc.scalar.copy)
+                group_e(n - EXP_LAG, 1, nc.scalar.copy)
 
             if live(n - MAX_LAG):
                 max_of(plain_max, n - MAX_LAG, capped, "plain_max")
                 max_of(turned_max, n - MAX_LAG, turned, "turned_max")
             if live(n - QUANT_LAG):
                 quantise_e(n - QUANT_LAG)
+            if live(n) or live(n - MAX_LAG):
+                capped[n] = sbuf("capped", [P, 2, PLAIN], F32)
             if live(n - MAX_LAG):
-                join_max(n - MAX_LAG)
+                join_max(n - MAX_LAG, capped[n])
             if live(n - NORM_LAG):
                 invert_sum(n - NORM_LAG)
+            if live(n - MAX_LAG):
+                scale_max(n - MAX_LAG)
             if part == 2:
                 if h == 0:
                     group_v(0)
@@ -372,22 +390,20 @@ def tile_naivesdpa_kernel(tc, query, key, value, attn_mask, out):
                 if next_head is not None:
                     quantise_v(next_head)
 
-            if live(n - MAX_LAG):
-                scale_max(n - MAX_LAG)
             if live(n):
                 add_plain_bias(n)
             if live(n - QUANT_LAG):
                 join_sum(n - QUANT_LAG)
 
-            if live(n - EXP_LAG):
-                group_e(n - EXP_LAG, 0)
+            if live(n - EXP_LAG) and live(n + 1):
+                group_e(n - EXP_LAG, 0, nc.vector.tensor_copy)
             if live(n - NORM_LAG):
                 divide_and_store(n - NORM_LAG)
-            if live(n - EXP_LAG):
-                group_e(n - EXP_LAG, 1)
+            if live(n - EXP_LAG) and live(n + 1):
+                group_e(n - EXP_LAG, 1, nc.vector.tensor_copy)
             if n < PAIRS_PER_HEAD:
                 turn_bias(n)
             if part == 2 and h + 2 < H:
-                load_head(k_raw, k_rows, h + 2, "k_raw")
-                load_head(q_raw, q_rows, h + 2, "q_raw")
+                load_tiles(k_raw, k_rows, h + 2, "k_raw", all_tiles)
+                load_tiles(q_raw, q_rows, h + 2, "q_raw", all_tiles)
                 load_v(h + 2)

@@ -55,8 +55,8 @@ SBUF_DEPTH = {
     "e_grouped": 3,
     "e_words": 2,
     "e_scales": 2,
-    "part_sum": QUANT_LAG - EXP_LAG + 2,
-    "row_sum": 2,
+    "part_sum": 2,
+    "row_sum": NORM_LAG - EXP_LAG + 1,
     "row_inv": 2,
     "out_sb": 2,
 }
@@ -139,6 +139,9 @@ def tile_naivesdpa_kernel(tc, query, key, value, attn_mask, out):
                     bias_raw[:, j, cols].rearrange("q (p i c) -> q i p c", i=2, c=2),
                     1.0 / SOFT_CAP,
                 )
+
+        def gpsimd_mul(out, in_, factor):
+            nc.gpsimd.tensor_scalar(out=out, in0=in_, scalar1=factor, scalar2=0.0, op0=ALU.mult, op1=ALU.add)
 
         def turn_bias(pair):
             bank = ps.tile([P, TURNED_TILES, 2 * P], F32, name="bias_turn", tag="t", bufs=TRANSPOSE_BANKS)
@@ -285,7 +288,10 @@ def tile_naivesdpa_kernel(tc, query, key, value, attn_mask, out):
                 in1=row_inv[pair][:].unsqueeze(2).to_broadcast([P, 2, D]),
                 op=ALU.mult,
             )
-            if part == PAIRS_PER_HEAD - 1:
+            if h == H - 1:
+                tiles = slice(2 * part, 2 * part + 2)
+                nc.sync.dma_start(out=out_rows[:, tiles, h, :], in_=out_sb[h][:, tiles, :])
+            elif part == PAIRS_PER_HEAD - 1:
                 nc.sync.dma_start(out=out_rows[:, :, h, :], in_=out_sb[h][:])
 
         def live(pair):
@@ -306,8 +312,9 @@ def tile_naivesdpa_kernel(tc, query, key, value, attn_mask, out):
         load_tiles(q_raw, q_rows, 0, "q_raw", q_rest)
         nc.sync.dma_start(out=bias_raw[:, 2:4, :], in_=bias_rows[:, 2:4, :])
         load_tiles(k_raw, k_rows, 1, "k_raw", all_tiles)
+        nc.sync.dma_start(out=bias_raw[:, 4:6, :], in_=bias_rows[:, 4:6, :])
         load_tiles(q_raw, q_rows, 1, "q_raw", all_tiles)
-        nc.sync.dma_start(out=bias_raw[:, 4:8, :], in_=bias_rows[:, 4:8, :])
+        nc.sync.dma_start(out=bias_raw[:, 6:8, :], in_=bias_rows[:, 6:8, :])
         load_v(0)
         load_v(1)
         ident = sb.tile([P, P], BF16, name="ident", tag="ident")
@@ -317,13 +324,15 @@ def tile_naivesdpa_kernel(tc, query, key, value, attn_mask, out):
         k_bank, q_bank = transpose_tiles(k_raw[0], k_first), transpose_tiles(q_raw[0], q_first)
         keep_k(0, k_bank, nc.vector.tensor_copy, k_first)
         keep_q(0, q_bank, nc.scalar.copy, q_first)
-        score_bank(0)
         keep_k(0, transpose_tiles(k_raw[0], k_rest), nc.vector.tensor_copy, k_rest)
-        for x in range(1, SCORE_BANKS):
+        for x in range(SCORE_BANKS):
             score_bank(x)
-        keep_q(0, transpose_tiles(q_raw[0], q_rest), nc.vector.tensor_copy, q_rest)
+        q_bank = transpose_tiles(q_raw[0], q_rest)
         scale_bias(0, nc.vector.tensor_scalar_mul)
         scale_bias(1, nc.vector.tensor_scalar_mul)
+        keep_q(0, q_bank, nc.vector.tensor_copy, q_rest)
+        scale_bias(2, gpsimd_mul)
+        scale_bias(3, nc.vector.tensor_scalar_mul)
 
         for n in range(NPAIR + NORM_LAG + 1):
             h, part = divmod(n, PAIRS_PER_HEAD)
@@ -342,12 +351,9 @@ def tile_naivesdpa_kernel(tc, query, key, value, attn_mask, out):
             if live(n):
                 tanh_bank(4 * n + 2)
                 tanh_bank(4 * n + 3)
-            if live(n - TURN_LAG):
+            if live(n - TURN_LAG) and n - TURN_LAG >= TURNED_BANKS:
                 add_turned_bias(n - TURN_LAG, 0)
                 add_turned_bias(n - TURN_LAG, 1)
-            if 1 <= n < PAIRS_PER_HEAD:
-                scale_bias(2 * n, nc.scalar.mul)
-                scale_bias(2 * n + 1, nc.scalar.mul)
             if live(n - NORM_LAG):
                 e_times_v(n - NORM_LAG)
             if live(n - EXP_LAG):
@@ -362,6 +368,9 @@ def tile_naivesdpa_kernel(tc, query, key, value, attn_mask, out):
                 exp_keys(n - EXP_LAG, 1, 0)
                 exp_keys(n - EXP_LAG, 1, 1)
                 transpose_e(n - EXP_LAG, 1)
+            if 2 <= n < PAIRS_PER_HEAD:
+                scale_bias(2 * n, nc.scalar.mul)
+                scale_bias(2 * n + 1, nc.scalar.mul)
             if live(n - EXP_LAG) and not live(n + 1):
                 group_e(n - EXP_LAG, 0, nc.scalar.copy)
                 group_e(n - EXP_LAG, 1, nc.scalar.copy)
@@ -392,8 +401,8 @@ def tile_naivesdpa_kernel(tc, query, key, value, attn_mask, out):
 
             if live(n):
                 add_plain_bias(n)
-            if live(n - QUANT_LAG):
-                join_sum(n - QUANT_LAG)
+            if live(n - EXP_LAG):
+                join_sum(n - EXP_LAG)
 
             if live(n - EXP_LAG) and live(n + 1):
                 group_e(n - EXP_LAG, 0, nc.vector.tensor_copy)
@@ -401,6 +410,9 @@ def tile_naivesdpa_kernel(tc, query, key, value, attn_mask, out):
                 divide_and_store(n - NORM_LAG)
             if live(n - EXP_LAG) and live(n + 1):
                 group_e(n - EXP_LAG, 1, nc.vector.tensor_copy)
+            if 0 <= n - 1 < TURNED_BANKS:
+                add_turned_bias(n - 1, 0)
+                add_turned_bias(n - 1, 1)
             if n < PAIRS_PER_HEAD:
                 turn_bias(n)
             if part == 2 and h + 2 < H:

import math
from contextlib import ExitStack

import concourse.mybir as mybir
from concourse.masks import make_identity

F32 = mybir.dt.float32
BF16 = mybir.dt.bfloat16
U32 = mybir.dt.uint32
U8 = mybir.dt.uint8
FP8X4 = mybir.dt.float8_e4m3fn_x4
ACT = mybir.ActivationFunctionType
ALU = mybir.AluOpType

P = 128
S = 1024
H = 16
D = 128
NT = S // P
BANK = 512
PACK = 4
PASSES = S // (P * PACK)
WORDS = S // 2
PAIRS_PER_HEAD = NT // 2
NPAIR = H * PAIRS_PER_HEAD
NBANK = 4 * NPAIR
SOFT_CAP = 20.0
FLOPS = 2 * 2 * H * S * S * D

TURNED_TILES = 2
TURNED = TURNED_TILES * P
PLAIN = S - TURNED

TURN_LAG = 2
MAX_LAG = 2
EXP_LAG = 3
QUANT_LAG = 4
NORM_LAG = 5

SBUF_DEPTH = {
    "k_raw": 3,
    "q_raw": 3,
    "v_raw": 3,
    "k_t": 2,
    "q_t": 2,
    "v_grouped": 2,
    "v_words": 3,
    "v_scales": 3,
    "tanh_sb": TURN_LAG + 3,
    "capped": EXP_LAG + 1,
    "plain_max": 2,
    "turned_max": 2,
    "exp_bias": 2,
    "e": 4,
    "e_grouped": 3,
    "e_words": 2,
    "e_scales": 2,
    "part_sum": 2,
    "row_sum": NORM_LAG - EXP_LAG + 1,
    "row_inv": 2,
    "out_sb": 2,
}
SCORE_BANKS = 3
TURNED_BANKS = 2
TRANSPOSE_BANKS = 2
OUT_BANKS = 1


def tile_naivesdpa_kernel(tc, query, key, value, attn_mask, out):
    nc = tc.nc
    q_rows = query.rearrange("b (j p) h d -> p (b j) h d", p=P)
    k_rows = key.rearrange("b (j p) h d -> p (b j) h d", p=P)
    v_rows = value.rearrange("b (g p t) h d -> p (b g) t h d", p=P, t=PACK)
    bias_rows = attn_mask.rearrange("a b (j p) k -> p (a b j) k", p=P)
    out_rows = out.rearrange("b (j p) h d -> p (b j) h d", p=P)
    tanh_scale = 1.0 / (math.sqrt(D) * SOFT_CAP)
    all_tiles = slice(0, NT)

    with ExitStack() as ctx:
        sb = ctx.enter_context(tc.tile_pool(name="sb", bufs=1))
        ps = ctx.enter_context(tc.psum_pool(name="ps", bufs=1))
        ctx.enter_context(tc.manual_schedule())

        k_raw, q_raw, v_raw, k_t, q_t, v_grouped, v_words, v_scales, out_sb = {}, {}, {}, {}, {}, {}, {}, {}, {}
        scores, tanh_sb, capped, turned, exp_bias, e_sb, e_t, e_grouped, e_words, e_scales = {}, {}, {}, {}, {}, {}, {}, {}, {}, {}
        plain_max, turned_max, neg_max, part_sum, row_sum, row_inv, out_ps = {}, {}, {}, {}, {}, {}, {}

        def sbuf(tag, shape, dtype):
            return sb.tile(shape, dtype, name=tag, tag=tag, bufs=SBUF_DEPTH[tag], align_bytes=64)

        def load_tiles(store, rows, h, tag, tiles):
            if tiles.start == 0:
                store[h] = sbuf(tag, [P, NT, D], BF16)
            nc.sync.dma_start(out=store[h][:, tiles, :], in_=rows[:, tiles, h, :])

        def load_v(h):
            v_raw[h] = sbuf("v_raw", [P, NT, D], BF16)
            for g in range(PASSES):
                nc.sync.dma_start(out=v_raw[h][:, PACK * g:PACK * (g + 1), :], in_=v_rows[:, g, :, h, :])

        def transpose_tiles(raw, tiles):
            count = tiles.stop - tiles.start
            bank = ps.tile([P, count * P], BF16, name="head_t", tag="t", bufs=TRANSPOSE_BANKS)
            for j in range(count):
                nc.tensor.transpose(bank[:, j * P:(j + 1) * P], raw[:, tiles.start + j, :], ident[:])
            return bank

        def keep_q(h, bank, copy, tiles):
            if tiles.start == 0:
                q_t[h] = sbuf("q_t", [P, S], BF16)
            copy(out=q_t[h][:, tiles.start * P:tiles.stop * P].bitcast(F32), in_=bank[:].bitcast(F32))

        def keep_k(h, bank, copy, tiles):
            if tiles.start == 0:
                k_t[h] = sbuf("k_t", [P, S], BF16)
            passes = (tiles.stop - tiles.start) // PACK
            copy(
                out=k_t[h][:, tiles.start * P:tiles.stop * P].bitcast(F32).rearrange("d (g i p) -> d g i p", g=passes, i=2),
                in_=bank[:].bitcast(F32).rearrange("d (g p i) -> d g i p", g=passes, i=2),
            )

        def group_v(h):
            v_grouped[h] = sbuf("v_grouped", [P, S], BF16)
            nc.vector.tensor_copy(
                out=v_grouped[h][:].rearrange("p (g d t) -> p g d t", g=PASSES, t=PACK),
                in_=v_raw[h][:].rearrange("p (g t) d -> p g d t", g=PASSES),
            )

        def quantise_v(h):
            v_words[h] = sbuf("v_words", [P, PASSES * D], U32)
            v_scales[h] = sbuf("v_scales", [P, PASSES * D], U8)
            nc.vector.quantize_mx(out=v_words[h][:].bitcast(FP8X4), scales=v_scales[h][:], in_=v_grouped[h][:])

        def scale_bias(j, mul):
            for g in range(PASSES):
                cols = slice(g * BANK, (g + 1) * BANK)
                mul(
                    b20[:, j, cols].rearrange("q (i p c) -> q i p c", i=2, c=2),
                    bias_raw[:, j, cols].rearrange("q (p i c) -> q i p c", i=2, c=2),
                    1.0 / SOFT_CAP,
                )

        def gpsimd_mul(out, in_, factor):
            nc.gpsimd.tensor_scalar(out=out, in0=in_, scalar1=factor, scalar2=0.0, op0=ALU.mult, op1=ALU.add)

        def turn_bias(pair):
            bank = ps.tile([P, TURNED_TILES, 2 * P], F32, name="bias_turn", tag="t", bufs=TRANSPOSE_BANKS)
            for u in range(2):
                for i in range(TURNED_TILES):
                    nc.tensor.transpose(
                        bank[:, i, u * P:(u + 1) * P], b20[:, 2 * pair + u, PLAIN + i * P:PLAIN + (i + 1) * P], ident_f32[:]
                    )
            nc.vector.tensor_copy(out=bias_t[:, :, 2 * P * pair:2 * P * (pair + 1)], in_=bank[:])

        def score_bank(x):
            pair, b = divmod(x, 4)
            h = pair // PAIRS_PER_HEAD
            tile_no = 2 * (pair % PAIRS_PER_HEAD) + b // 2
            q_tile = q_t[h][:, tile_no * P:(tile_no + 1) * P]
            scores[x] = ps.tile([P, BANK], F32, name="scores", tag="scores", bufs=SCORE_BANKS)
            if b % 2 == 0:
                nc.tensor.matmul(scores[x][:], lhsT=q_tile, rhs=k_t[h][:, 0:BANK], start=True, stop=True)
            else:
                nc.tensor.matmul(
                    scores[x][:, 0:PLAIN - BANK], lhsT=q_tile, rhs=k_t[h][:, BANK:PLAIN], start=True, stop=True
                )
                for i in range(TURNED_TILES):
                    nc.tensor.matmul(
                        scores[x][:, PLAIN - BANK + i * P:PLAIN - BANK + (i + 1) * P],
                        lhsT=k_t[h][:, PLAIN + i * P:PLAIN + (i + 1) * P],
                        rhs=q_tile,
                        start=True,
                        stop=True,
                    )

        def tanh_bank(x):
            pair, b = divmod(x, 4)
            half = b % 2
            nc.scalar.activation(
                out=tanh_sb[pair][:, b // 2, half * BANK:(half + 1) * BANK], in_=scores[x][:], func=ACT.Tanh, scale=tanh_scale
            )
            if x + SCORE_BANKS < NBANK:
                score_bank(x + SCORE_BANKS)

        def add_plain_bias(pair):
            j = 2 * (pair % PAIRS_PER_HEAD)
            nc.gpsimd.tensor_tensor(
                out=capped[pair][:], in0=tanh_sb[pair][:, :, 0:PLAIN], in1=b20[:, j:j + 2, 0:PLAIN], op=ALU.add
            )

        def add_turned_bias(pair, u):
            if u == 0:
                turned[pair] = ps.tile([P, 2, TURNED], F32, name="turned", tag="turned", bufs=TURNED_BANKS)
            tile_no = 2 * (pair % PAIRS_PER_HEAD) + u
            for i in range(TURNED_TILES):
                total = turned[pair][:, u, i * P:(i + 1) * P]
                bias_tile = bias_t[:, i, tile_no * P:(tile_no + 1) * P]
                tanh_tile = tanh_sb[pair][:, u, PLAIN + i * P:PLAIN + (i + 1) * P]
                nc.tensor.matmul(total, lhsT=bias_tile, rhs=ident_f32[:], is_transpose=True, start=True, stop=False)
                nc.tensor.matmul(total, lhsT=tanh_tile, rhs=ident_f32[:], is_transpose=True, start=False, stop=True)

        def max_of(store, pair, source, tag):
            store[pair] = sbuf(tag, [P, 2, 1], F32)
            nc.vector.tensor_reduce(
                out=store[pair][:, :, 0], in_=source[pair][:], axis=mybir.AxisListType.X, op=ALU.max, negate=True
            )

        def join_max(pair, host):
            neg_max[pair] = host[:, :, 0:1]
            nc.vector.tensor_tensor(out=neg_max[pair], in0=plain_max[pair][:], in1=turned_max[pair][:], op=ALU.min)

        def scale_max(pair):
            exp_bias[pair] = sbuf("exp_bias", [P, 2, 1], F32)
            nc.vector.tensor_scalar_mul(exp_bias[pair][:], neg_max[pair], SOFT_CAP)

        def exp_keys(pair, u, part):
            if part == 0:
                if u == 0:
                    part_sum[pair] = sbuf("part_sum", [P, 2, 2], F32)
                e_sb[(pair, u)] = sbuf("e", [P, S], BF16)
            nc.scalar.activation(
                out=e_sb[(pair, u)][:, slice(0, PLAIN) if part == 0 else slice(PLAIN, S)],
                in_=(capped if part == 0 else turned)[pair][:, u, :],
                func=ACT.Exp,
                bias=exp_bias[pair][:, u, :],
                scale=SOFT_CAP,
                accum_out=part_sum[pair][:, u, part:part + 1],
            )

        def transpose_e(pair, u):
            e_t[(pair, u)] = ps.tile([P, WORDS], F32, name="e_t", tag="t", bufs=TRANSPOSE_BANKS)
            words = e_sb[(pair, u)][:].bitcast(F32)
            for block in range(WORDS // P):
                cols = slice(block * P, (block + 1) * P)
                nc.tensor.transpose(e_t[(pair, u)][:, cols], words[:, cols], ident_f32[:])

        def group_e(pair, u, copy):
            if u == 0:
                e_grouped[pair] = sbuf("e_grouped", [P, 2, S], BF16)
            copy(
                out=e_grouped[pair][:, u, :].bitcast(F32).rearrange("p (g q i) -> p g q i", g=PASSES, i=2),
                in_=e_t[(pair, u)][:].rearrange("p (g i q) -> p g q i", g=PASSES, i=2),
            )

        def quantise_e(pair):
            e_words[pair] = sbuf("e_words", [P, 2 * PASSES * P], U32)
            e_scales[pair] = sbuf("e_scales", [P, 2 * PASSES * P], U8)
            nc.vector.quantize_mx(
                out=e_words[pair][:].bitcast(FP8X4),
                scales=e_scales[pair][:],
                in_=e_grouped[pair][:].rearrange("p u c -> p (u c)"),
            )

        def e_times_v(pair):
            h = pair // PAIRS_PER_HEAD
            out_ps[pair] = ps.tile([P, 2, D], F32, name="out_ps", tag="out_ps", bufs=OUT_BANKS)
            for u in range(2):
                for g in range(PASSES):
                    q_cols = slice((PASSES * u + g) * P, (PASSES * u + g + 1) * P)
                    d_cols = slice(g * D, (g + 1) * D)
                    nc.tensor.matmul_mx(
                        out=out_ps[pair][:, u, :],
                        lhsT=e_words[pair][:, q_cols].bitcast(FP8X4),
                        lhsT_scale=e_scales[pair][:, q_cols],
                        rhs=v_words[h][:, d_cols].bitcast(FP8X4),
                        rhs_scale=v_scales[h][:, d_cols],
                        start=(g == 0),
                        stop=(g == PASSES - 1),
                    )

        def join_sum(pair):
            row_sum[pair] = sbuf("row_sum", [P, 2], F32)
            nc.gpsimd.tensor_tensor(
                out=row_sum[pair][:], in0=part_sum[pair][:, :, 0], in1=part_sum[pair][:, :, 1], op=ALU.add
            )

        def invert_sum(pair):
            row_inv[pair] = sbuf("row_inv", [P, 2], F32)
            nc.vector.reciprocal(row_inv[pair][:], row_sum[pair][:])

        def divide_and_store(pair):
            h, part = divmod(pair, PAIRS_PER_HEAD)
            if part == 0:
                out_sb[h] = sbuf("out_sb", [P, NT, D], F32)
            nc.vector.tensor_tensor(
                out=out_sb[h][:, 2 * part:2 * part + 2, :],
                in0=out_ps[pair][:],
                in1=row_inv[pair][:].unsqueeze(2).to_broadcast([P, 2, D]),
                op=ALU.mult,
            )
            if h == H - 1:
                tiles = slice(2 * part, 2 * part + 2)
                nc.sync.dma_start(out=out_rows[:, tiles, h, :], in_=out_sb[h][:, tiles, :])
            elif part == PAIRS_PER_HEAD - 1:
                nc.sync.dma_start(out=out_rows[:, :, h, :], in_=out_sb[h][:])

        def live(pair):
            return 0 <= pair < NPAIR

        warm = sb.tile([P, 2], F32, name="warm", tag="warm")
        nc.vector.memset(warm[:, 0:1], 0.0)
        nc.scalar.activation(out=warm[:, 1:2], in_=warm[:, 0:1], func=ACT.Tanh)
        bias_raw = sb.tile([P, NT, S], BF16, name="bias_raw", tag="bias_raw")
        b20 = sb.tile([P, NT, S], F32, name="b20", tag="b20")
        bias_t = sb.tile([P, TURNED_TILES, S], F32, name="bias_t", tag="bias_t")
        k_first, k_rest = slice(0, PACK), slice(PACK, NT)
        q_first, q_rest = slice(0, 2), slice(2, NT)
        load_tiles(k_raw, k_rows, 0, "k_raw", k_first)
        load_tiles(q_raw, q_rows, 0, "q_raw", q_first)
        load_tiles(k_raw, k_rows, 0, "k_raw", k_rest)
        nc.sync.dma_start(out=bias_raw[:, 0:2, :], in_=bias_rows[:, 0:2, :])
        load_tiles(q_raw, q_rows, 0, "q_raw", q_rest)
        nc.sync.dma_start(out=bias_raw[:, 2:4, :], in_=bias_rows[:, 2:4, :])
        load_tiles(k_raw, k_rows, 1, "k_raw", all_tiles)
        nc.sync.dma_start(out=bias_raw[:, 4:6, :], in_=bias_rows[:, 4:6, :])
        load_tiles(q_raw, q_rows, 1, "q_raw", all_tiles)
        nc.sync.dma_start(out=bias_raw[:, 6:8, :], in_=bias_rows[:, 6:8, :])
        load_v(0)
        load_v(1)
        ident = sb.tile([P, P], BF16, name="ident", tag="ident")
        make_identity(nc, ident[:])
        ident_f32 = sb.tile([P, P], F32, name="ident_f32", tag="ident_f32")
        make_identity(nc, ident_f32[:])
        k_bank, q_bank = transpose_tiles(k_raw[0], k_first), transpose_tiles(q_raw[0], q_first)
        keep_k(0, k_bank, nc.vector.tensor_copy, k_first)
        keep_q(0, q_bank, nc.scalar.copy, q_first)
        keep_k(0, transpose_tiles(k_raw[0], k_rest), nc.vector.tensor_copy, k_rest)
        for x in range(SCORE_BANKS):
            score_bank(x)
        q_bank = transpose_tiles(q_raw[0], q_rest)
        scale_bias(0, nc.vector.tensor_scalar_mul)
        scale_bias(1, nc.vector.tensor_scalar_mul)
        keep_q(0, q_bank, nc.vector.tensor_copy, q_rest)
        scale_bias(2, gpsimd_mul)
        scale_bias(3, nc.vector.tensor_scalar_mul)

        for n in range(NPAIR + NORM_LAG + 1):
            h, part = divmod(n, PAIRS_PER_HEAD)
            next_head = h + 1 if h + 1 < H else None

            if live(n):
                tanh_sb[n] = sbuf("tanh_sb", [P, 2, S], F32)
                tanh_bank(4 * n)
                tanh_bank(4 * n + 1)
            new_k = next_head is not None and part == 1
            new_q = next_head is not None and part == 2
            if new_k:
                head_bank = transpose_tiles(k_raw[next_head], all_tiles)
            if new_q:
                head_bank = transpose_tiles(q_raw[next_head], all_tiles)
            if live(n):
                tanh_bank(4 * n + 2)
                tanh_bank(4 * n + 3)
            if live(n - TURN_LAG) and n - TURN_LAG >= TURNED_BANKS:
                add_turned_bias(n - TURN_LAG, 0)
                add_turned_bias(n - TURN_LAG, 1)
            if live(n - NORM_LAG):
                e_times_v(n - NORM_LAG)
            if live(n - EXP_LAG):
                exp_keys(n - EXP_LAG, 0, 0)
            if new_k:
                keep_k(next_head, head_bank, nc.scalar.copy, all_tiles)
            if new_q:
                keep_q(next_head, head_bank, nc.scalar.copy, all_tiles)
            if live(n - EXP_LAG):
                exp_keys(n - EXP_LAG, 0, 1)
                transpose_e(n - EXP_LAG, 0)
                exp_keys(n - EXP_LAG, 1, 0)
                exp_keys(n - EXP_LAG, 1, 1)
                transpose_e(n - EXP_LAG, 1)
            if 2 <= n < PAIRS_PER_HEAD:
                scale_bias(2 * n, nc.scalar.mul)
                scale_bias(2 * n + 1, nc.scalar.mul)
            if live(n - EXP_LAG) and not live(n + 1):
                group_e(n - EXP_LAG, 0, nc.scalar.copy)
                group_e(n - EXP_LAG, 1, nc.scalar.copy)

            if live(n - MAX_LAG):
                max_of(plain_max, n - MAX_LAG, capped, "plain_max")
                max_of(turned_max, n - MAX_LAG, turned, "turned_max")
            if live(n - QUANT_LAG):
                quantise_e(n - QUANT_LAG)
            if live(n) or live(n - MAX_LAG):
                capped[n] = sbuf("capped", [P, 2, PLAIN], F32)
            if live(n - MAX_LAG):
                join_max(n - MAX_LAG, capped[n])
            if live(n - NORM_LAG):
                invert_sum(n - NORM_LAG)
            if live(n - MAX_LAG):
                scale_max(n - MAX_LAG)
            if part == 2:
                if h == 0:
                    group_v(0)
                if next_head is not None:
                    group_v(next_head)
            if part == 3:
                if h == 0:
                    quantise_v(0)
                if next_head is not None:
                    quantise_v(next_head)

            if live(n):
                add_plain_bias(n)
            if live(n - EXP_LAG):
                join_sum(n - EXP_LAG)

            if live(n - EXP_LAG) and live(n + 1):
                group_e(n - EXP_LAG, 0, nc.vector.tensor_copy)
            if live(n - NORM_LAG):
                divide_and_store(n - NORM_LAG)
            if live(n - EXP_LAG) and live(n + 1):
                group_e(n - EXP_LAG, 1, nc.vector.tensor_copy)
            if 0 <= n - 1 < TURNED_BANKS:
                add_turned_bias(n - 1, 0)
                add_turned_bias(n - 1, 1)
            if n < PAIRS_PER_HEAD:
                turn_bias(n)
            if part == 2 and h + 2 < H:
                load_tiles(k_raw, k_rows, h + 2, "k_raw", all_tiles)
                load_tiles(q_raw, q_rows, h + 2, "q_raw", all_tiles)
                load_v(h + 2)
